import numpy as np
import ml_dtypes

BF16 = ml_dtypes.bfloat16


def bf(x):
    return np.asarray(x, np.float32).astype(BF16)


def f32(x):
    return np.asarray(x, np.float32)


def f64(x):
    return np.asarray(x).astype(np.float64)


def striped(idx):
    return np.tile(idx.reshape(-1, 16).T, (8, 1))


C, S, N = 512, 1024, 2048
EPS = 1e-5


def setup_inputs():
    return {"tok": f32(np.random.standard_normal((C, S))), "pos": f32(np.random.standard_normal((C, N))), "gain": f32(1.0 + 0.1 * np.random.standard_normal((C, 1))), "bias": f32(0.1 * np.random.standard_normal((C, 1))), "offs": striped(np.random.permutation(np.tile(np.arange(S), 2))[:N])}


def reference(tok, pos, gain, bias, offs):
    idx = offs[:16].T.reshape(-1)
    x = f64(tok)[:, idx] + f64(pos)
    mu = x.mean(axis=0, keepdims=True)
    xc = x - mu
    var = (xc * xc).mean(axis=0, keepdims=True)
    return xc / np.sqrt(var + EPS) * f64(gain) + f64(bias)

@@ -1,0 +1,103 @@
+import concourse.mybir as mybir
+from concourse.masks import make_identity
+
+F32 = mybir.dt.float32
+U16 = mybir.dt.uint16
+ADD = mybir.AluOpType.add
+MULT = mybir.AluOpType.mult
+IDENTITY = mybir.ActivationFunctionType.Identity
+SQRT = mybir.ActivationFunctionType.Sqrt
+
+P = 128
+C, S, N = 512, 1024, 2048
+BLOCKS = C // P
+PIECE = 512
+PIECES = N // PIECE
+GROUPS = PIECE // P
+EPS = 1e-5
+
+
+def tile_proteintransformer_kernel(tc, tok, pos, gain, bias, offs, out):
+    nc = tc.nc
+    with (
+        tc.tile_pool(name="held", bufs=1) as held,
+        tc.tile_pool(name="summed", bufs=2) as summed,
+        tc.tile_pool(name="stats", bufs=4) as stats,
+        tc.tile_pool(name="normed", bufs=3) as normed,
+        tc.tile_pool(name="result", bufs=4) as result,
+        tc.psum_pool(name="flipped", bufs=4) as flipped,
+        tc.psum_pool(name="restored", bufs=4) as restored,
+    ):
+        offsets = held.tile([P, N // 16], U16, name="offsets")
+        nc.sync.dma_start(offsets[:], offs)
+        tok_sb = [held.tile([P, S], F32, name=f"tok{b}") for b in range(BLOCKS)]
+        pos_sb = [
+            [held.tile([P, PIECE], F32, name=f"pos{b}_{k}") for k in range(PIECES)]
+            for b in range(BLOCKS)
+        ]
+        for b in range(BLOCKS):
+            nc.sync.dma_start(tok_sb[b][:], tok[b * P : (b + 1) * P, :])
+            nc.scalar.dma_start(pos_sb[b][0][:], pos[b * P : (b + 1) * P, 0:PIECE])
+        for k in range(1, PIECES):
+            for b in range(BLOCKS):
+                nc.sync.dma_start(
+                    pos_sb[b][k][:],
+                    pos[b * P : (b + 1) * P, k * PIECE : (k + 1) * PIECE],
+                )
+
+        identity = held.tile([P, P], F32, name="identity")
+        make_identity(nc, identity[:])
+        eps = held.tile([P, 1], F32, name="eps")
+        nc.gpsimd.memset(eps[:], EPS)
+
+        rows = held.tile([P, P], F32, name="rows")
+        nc.gpsimd.memset(rows[:], 0.0)
+        nc.scalar.dma_start(rows[0:BLOCKS, :], gain.rearrange("(b p) o -> b (p o)", p=P))
+        nc.scalar.dma_start(
+            rows[BLOCKS : 2 * BLOCKS, :], bias.rearrange("(b p) o -> b (p o)", p=P)
+        )
+        rows_t = flipped.tile([P, P], F32, name="rows_t", tag="x_t")
+        nc.tensor.transpose(rows_t[:], rows[:], identity[:])
+        affine = held.tile([P, 2 * BLOCKS], F32, name="affine")
+        nc.scalar.copy(affine[:], rows_t[:, 0 : 2 * BLOCKS])
+
+        for k in range(PIECES):
+            piece_offsets = offsets[:, k * (PIECE // 16) : (k + 1) * (PIECE // 16)]
+            x = [summed.tile([P, PIECE], F32, name=f"x{b}") for b in range(BLOCKS)]
+            for b in range(BLOCKS):
+                nc.vector.tensor_tensor(
+                    x[b][:], tok_sb[b][:].indirect(piece_offsets), pos_sb[b][k][:], ADD
+                )
+
+            y = [restored.tile([P, PIECE], F32, name=f"y{b}", tag="y") for b in range(BLOCKS)]
+            for g in range(GROUPS):
+                cols = slice(g * P, (g + 1) * P)
+                x_t = flipped.tile([P, C], F32, name="x_t")
+                for b in range(BLOCKS):
+                    nc.tensor.transpose(x_t[:, b * P : (b + 1) * P], x[b][:, cols], identity[:])
+                six = stats.tile([P, 6], F32, name="six")
+                nc.vector.bn_stats(six[:], x_t[:])
+                mean_var = stats.tile([P, 2], F32, name="mean_var")
+                nc.vector.bn_aggr(mean_var[:], six[:])
+                rstd = stats.tile([P, 1], F32, name="rstd")
+                nc.scalar.activation(rstd[:], mean_var[:, 1:2], SQRT, bias=eps[:])
+                nc.vector.reciprocal(rstd[:], rstd[:])
+                shift = stats.tile([P, 1], F32, name="shift")
+                nc.vector.tensor_scalar(shift[:], mean_var[:, 0:1], -1.0, rstd[:], MULT, MULT)
+                y_t = normed.tile([P, C], F32, name="y_t")
+                nc.scalar.activation(y_t[:], x_t[:], IDENTITY, bias=shift[:], scale=rstd[:])
+                for b in range(BLOCKS):
+                    nc.tensor.transpose(y[b][:, cols], y_t[:, b * P : (b + 1) * P], identity[:])
+
+            for b in range(BLOCKS):
+                o = result.tile([P, PIECE], F32, name="o")
+                nc.scalar.activation(
+                    o[:],
+                    y[b][:],
+                    IDENTITY,
+                    bias=affine[:, BLOCKS + b : BLOCKS + b + 1],
+                    scale=affine[:, b : b + 1],
+                )
+                nc.sync.dma_start(
+                    out[b * P : (b + 1) * P, k * PIECE : (k + 1) * PIECE], o[:]
+                )

@@ -4,9 +4,8 @@ from concourse.masks import make_identity
 F32 = mybir.dt.float32
 U16 = mybir.dt.uint16
 ADD = mybir.AluOpType.add
-MULT = mybir.AluOpType.mult
 IDENTITY = mybir.ActivationFunctionType.Identity
-SQRT = mybir.ActivationFunctionType.Sqrt
+RSQRT = mybir.ActivationFunctionType.Abs_reciprocal_sqrt
 
 P = 128
 C, S, N = 512, 1024, 2048
@@ -14,6 +13,7 @@ BLOCKS = C // P
 PIECE = 512
 PIECES = N // PIECE
 GROUPS = PIECE // P
+AHEAD = BLOCKS // GROUPS
 EPS = 1e-5
 
 
@@ -28,6 +28,18 @@ def tile_proteintransformer_kernel(tc, tok, pos, gain, bias, offs, out):
         tc.psum_pool(name="flipped", bufs=4) as flipped,
         tc.psum_pool(name="restored", bufs=4) as restored,
     ):
+        identity = held.tile([P, P], F32, name="identity")
+        make_identity(nc, identity[:])
+        eps = held.tile([P, 1], F32, name="eps")
+        nc.gpsimd.memset(eps[:], EPS)
+
+        rows = held.tile([P, P], F32, name="rows")
+        nc.gpsimd.memset(rows[:], 0.0)
+        nc.scalar.dma_start(rows[0:BLOCKS, :], gain.rearrange("(b p) o -> b (p o)", p=P))
+        nc.scalar.dma_start(
+            rows[BLOCKS : 2 * BLOCKS, :], bias.rearrange("(b p) o -> b (p o)", p=P)
+        )
+
         offsets = held.tile([P, N // 16], U16, name="offsets")
         nc.sync.dma_start(offsets[:], offs)
         tok_sb = [held.tile([P, S], F32, name=f"tok{b}") for b in range(BLOCKS)]
@@ -40,38 +52,38 @@ def tile_proteintransformer_kernel(tc, tok, pos, gain, bias, offs, out):
             nc.scalar.dma_start(pos_sb[b][0][:], pos[b * P : (b + 1) * P, 0:PIECE])
         for k in range(1, PIECES):
             for b in range(BLOCKS):
-                nc.sync.dma_start(
+                queue = nc.sync if b % 2 == 0 else nc.scalar
+                queue.dma_start(
                     pos_sb[b][k][:],
                     pos[b * P : (b + 1) * P, k * PIECE : (k + 1) * PIECE],
                 )
 
-        identity = held.tile([P, P], F32, name="identity")
-        make_identity(nc, identity[:])
-        eps = held.tile([P, 1], F32, name="eps")
-        nc.gpsimd.memset(eps[:], EPS)
+        def look_up(x, k, b):
+            nc.vector.tensor_tensor(
+                x[b][:],
+                tok_sb[b][:].indirect(offsets[:, k * (PIECE // 16) : (k + 1) * (PIECE // 16)]),
+                pos_sb[b][k][:],
+                ADD,
+            )
 
-        rows = held.tile([P, P], F32, name="rows")
-        nc.gpsimd.memset(rows[:], 0.0)
-        nc.scalar.dma_start(rows[0:BLOCKS, :], gain.rearrange("(b p) o -> b (p o)", p=P))
-        nc.scalar.dma_start(
-            rows[BLOCKS : 2 * BLOCKS, :], bias.rearrange("(b p) o -> b (p o)", p=P)
-        )
+        x = [summed.tile([P, PIECE], F32, name=f"x{b}") for b in range(BLOCKS)]
+        for b in range(BLOCKS):
+            look_up(x, 0, b)
+
         rows_t = flipped.tile([P, P], F32, name="rows_t", tag="x_t")
         nc.tensor.transpose(rows_t[:], rows[:], identity[:])
         affine = held.tile([P, 2 * BLOCKS], F32, name="affine")
         nc.scalar.copy(affine[:], rows_t[:, 0 : 2 * BLOCKS])
 
         for k in range(PIECES):
-            piece_offsets = offsets[:, k * (PIECE // 16) : (k + 1) * (PIECE // 16)]
-            x = [summed.tile([P, PIECE], F32, name=f"x{b}") for b in range(BLOCKS)]
-            for b in range(BLOCKS):
-                nc.vector.tensor_tensor(
-                    x[b][:], tok_sb[b][:].indirect(piece_offsets), pos_sb[b][k][:], ADD
-                )
-
-            y = [restored.tile([P, PIECE], F32, name=f"y{b}", tag="y") for b in range(BLOCKS)]
+            if k + 1 < PIECES:
+                x_next = [summed.tile([P, PIECE], F32, name=f"x{b}") for b in range(BLOCKS)]
             for g in range(GROUPS):
+                if k + 1 < PIECES:
+                    for b in range(g * AHEAD, (g + 1) * AHEAD):
+                        look_up(x_next, k + 1, b)
                 cols = slice(g * P, (g + 1) * P)
+                first = k * PIECE + g * P
                 x_t = flipped.tile([P, C], F32, name="x_t")
                 for b in range(BLOCKS):
                     nc.tensor.transpose(x_t[:, b * P : (b + 1) * P], x[b][:, cols], identity[:])
@@ -79,25 +91,28 @@ def tile_proteintransformer_kernel(tc, tok, pos, gain, bias, offs, out):
                 nc.vector.bn_stats(six[:], x_t[:])
                 mean_var = stats.tile([P, 2], F32, name="mean_var")
                 nc.vector.bn_aggr(mean_var[:], six[:])
+                neg_mean = stats.tile([P, 1], F32, name="neg_mean")
+                nc.scalar.mul(neg_mean[:], mean_var[:, 0:1], -1.0)
                 rstd = stats.tile([P, 1], F32, name="rstd")
-                nc.scalar.activation(rstd[:], mean_var[:, 1:2], SQRT, bias=eps[:])
-                nc.vector.reciprocal(rstd[:], rstd[:])
+                nc.scalar.activation(rstd[:], mean_var[:, 1:2], RSQRT, bias=eps[:])
                 shift = stats.tile([P, 1], F32, name="shift")
-                nc.vector.tensor_scalar(shift[:], mean_var[:, 0:1], -1.0, rstd[:], MULT, MULT)
+                nc.scalar.activation(shift[:], neg_mean[:], IDENTITY, scale=rstd[:])
                 y_t = normed.tile([P, C], F32, name="y_t")
                 nc.scalar.activation(y_t[:], x_t[:], IDENTITY, bias=shift[:], scale=rstd[:])
+                y = restored.tile([P, BLOCKS, P], F32, name="y")
                 for b in range(BLOCKS):
-                    nc.tensor.transpose(y[b][:, cols], y_t[:, b * P : (b + 1) * P], identity[:])
-
-            for b in range(BLOCKS):
-                o = result.tile([P, PIECE], F32, name="o")
-                nc.scalar.activation(
-                    o[:],
-                    y[b][:],
-                    IDENTITY,
-                    bias=affine[:, BLOCKS + b : BLOCKS + b + 1],
-                    scale=affine[:, b : b + 1],
-                )
+                    nc.tensor.transpose(y[:, b, :], y_t[:, b * P : (b + 1) * P], identity[:])
+                o = result.tile([P, BLOCKS, P], F32, name="o")
+                for b in range(BLOCKS):
+                    nc.scalar.activation(
+                        o[:, b, :],
+                        y[:, b, :],
+                        IDENTITY,
+                        bias=affine[:, BLOCKS + b : BLOCKS + b + 1],
+                        scale=affine[:, b : b + 1],
+                    )
                 nc.sync.dma_start(
-                    out[b * P : (b + 1) * P, k * PIECE : (k + 1) * PIECE], o[:]
+                    out[:, first : first + P].rearrange("(b p) j -> p b j", p=P), o[:]
                 )
+            if k + 1 < PIECES:
+                x = x_next

@@ -12,8 +12,8 @@ C, S, N = 512, 1024, 2048
 BLOCKS = C // P
 PIECE = 512
 PIECES = N // PIECE
-GROUPS = PIECE // P
-AHEAD = BLOCKS // GROUPS
+GROUPS = N // P
+IN_PIECE = PIECE // P
 EPS = 1e-5
 
 
@@ -58,61 +58,92 @@ def tile_proteintransformer_kernel(tc, tok, pos, gain, bias, offs, out):
                     pos[b * P : (b + 1) * P, k * PIECE : (k + 1) * PIECE],
                 )
 
-        def look_up(x, k, b):
+        x, x_t, six, mean_var, neg_mean, rstd, shift, y_t, y, o = ({} for i in range(10))
+
+        def look_up(k, b):
+            if b == 0:
+                x[k] = [summed.tile([P, PIECE], F32, name=f"x{i}") for i in range(BLOCKS)]
             nc.vector.tensor_tensor(
-                x[b][:],
+                x[k][b][:],
                 tok_sb[b][:].indirect(offsets[:, k * (PIECE // 16) : (k + 1) * (PIECE // 16)]),
                 pos_sb[b][k][:],
                 ADD,
             )
 
-        x = [summed.tile([P, PIECE], F32, name=f"x{b}") for b in range(BLOCKS)]
+        def flip(g):
+            cols = slice(g % IN_PIECE * P, (g % IN_PIECE + 1) * P)
+            x_t[g] = flipped.tile([P, C], F32, name="x_t")
+            for b in range(BLOCKS):
+                nc.tensor.transpose(
+                    x_t[g][:, b * P : (b + 1) * P], x[g // IN_PIECE][b][:, cols], identity[:]
+                )
+
+        def flip_back(g):
+            y[g] = restored.tile([P, BLOCKS, P], F32, name="y")
+            for b in range(BLOCKS):
+                nc.tensor.transpose(y[g][:, b, :], y_t[g][:, b * P : (b + 1) * P], identity[:])
+
+        def gain_and_bias(g, b):
+            nc.scalar.activation(
+                o[g][:, b, :],
+                y[g][:, b, :],
+                IDENTITY,
+                bias=affine[:, BLOCKS + b : BLOCKS + b + 1],
+                scale=affine[:, b : b + 1],
+            )
+
         for b in range(BLOCKS):
-            look_up(x, 0, b)
+            look_up(0, b)
 
         rows_t = flipped.tile([P, P], F32, name="rows_t", tag="x_t")
         nc.tensor.transpose(rows_t[:], rows[:], identity[:])
         affine = held.tile([P, 2 * BLOCKS], F32, name="affine")
         nc.scalar.copy(affine[:], rows_t[:, 0 : 2 * BLOCKS])
 
-        for k in range(PIECES):
-            if k + 1 < PIECES:
-                x_next = [summed.tile([P, PIECE], F32, name=f"x{b}") for b in range(BLOCKS)]
-            for g in range(GROUPS):
-                if k + 1 < PIECES:
-                    for b in range(g * AHEAD, (g + 1) * AHEAD):
-                        look_up(x_next, k + 1, b)
-                cols = slice(g * P, (g + 1) * P)
-                first = k * PIECE + g * P
-                x_t = flipped.tile([P, C], F32, name="x_t")
-                for b in range(BLOCKS):
-                    nc.tensor.transpose(x_t[:, b * P : (b + 1) * P], x[b][:, cols], identity[:])
-                six = stats.tile([P, 6], F32, name="six")
-                nc.vector.bn_stats(six[:], x_t[:])
-                mean_var = stats.tile([P, 2], F32, name="mean_var")
-                nc.vector.bn_aggr(mean_var[:], six[:])
-                neg_mean = stats.tile([P, 1], F32, name="neg_mean")
-                nc.scalar.mul(neg_mean[:], mean_var[:, 0:1], -1.0)
-                rstd = stats.tile([P, 1], F32, name="rstd")
-                nc.scalar.activation(rstd[:], mean_var[:, 1:2], RSQRT, bias=eps[:])
-                shift = stats.tile([P, 1], F32, name="shift")
-                nc.scalar.activation(shift[:], neg_mean[:], IDENTITY, scale=rstd[:])
-                y_t = normed.tile([P, C], F32, name="y_t")
-                nc.scalar.activation(y_t[:], x_t[:], IDENTITY, bias=shift[:], scale=rstd[:])
-                y = restored.tile([P, BLOCKS, P], F32, name="y")
-                for b in range(BLOCKS):
-                    nc.tensor.transpose(y[:, b, :], y_t[:, b * P : (b + 1) * P], identity[:])
-                o = result.tile([P, BLOCKS, P], F32, name="o")
-                for b in range(BLOCKS):
-                    nc.scalar.activation(
-                        o[:, b, :],
-                        y[:, b, :],
-                        IDENTITY,
-                        bias=affine[:, BLOCKS + b : BLOCKS + b + 1],
-                        scale=affine[:, b : b + 1],
-                    )
-                nc.sync.dma_start(
-                    out[:, first : first + P].rearrange("(b p) j -> p b j", p=P), o[:]
+        for turn in range(GROUPS + 4):
+            flipping, measuring, scaling, restoring, finishing = (turn - i for i in range(5))
+
+            if 0 <= restoring < GROUPS:
+                flip_back(restoring)
+            if flipping < GROUPS:
+                flip(flipping)
+
+            if 0 <= measuring < GROUPS:
+                six[measuring] = stats.tile([P, 6], F32, name="six")
+                nc.vector.bn_stats(six[measuring][:], x_t[measuring][:])
+            if turn < GROUPS - IN_PIECE:
+                look_up(turn // IN_PIECE + 1, turn % IN_PIECE)
+            if 0 <= measuring < GROUPS:
+                mean_var[measuring] = stats.tile([P, 2], F32, name="mean_var")
+                nc.vector.bn_aggr(mean_var[measuring][:], six[measuring][:])
+
+            if 0 <= scaling < GROUPS:
+                neg_mean[scaling] = stats.tile([P, 1], F32, name="neg_mean")
+                nc.scalar.mul(neg_mean[scaling][:], mean_var[scaling][:, 0:1], -1.0)
+                rstd[scaling] = stats.tile([P, 1], F32, name="rstd")
+                nc.scalar.activation(rstd[scaling][:], mean_var[scaling][:, 1:2], RSQRT, bias=eps[:])
+            if 0 <= finishing < GROUPS:
+                o[finishing] = result.tile([P, BLOCKS, P], F32, name="o")
+                gain_and_bias(finishing, 0)
+                gain_and_bias(finishing, 1)
+            if 0 <= scaling < GROUPS:
+                shift[scaling] = stats.tile([P, 1], F32, name="shift")
+                nc.scalar.activation(
+                    shift[scaling][:], neg_mean[scaling][:], IDENTITY, scale=rstd[scaling][:]
                 )
-            if k + 1 < PIECES:
-                x = x_next
+            if 0 <= finishing < GROUPS:
+                gain_and_bias(finishing, 2)
+                gain_and_bias(finishing, 3)
+                nc.sync.dma_start(
+                    out[:, finishing * P : (finishing + 1) * P].rearrange("(b p) j -> p b j", p=P),
+                    o[finishing][:],
+                )
+            if 0 <= scaling < GROUPS:
+                y_t[scaling] = normed.tile([P, C], F32, name="y_t")
+                nc.scalar.activation(
+                    y_t[scaling][:],
+                    x_t[scaling][:],
+                    IDENTITY,
+                    bias=shift[scaling][:],
+                    scale=rstd[scaling][:],
+                )

@@ -10,8 +10,10 @@ RSQRT = mybir.ActivationFunctionType.Abs_reciprocal_sqrt
 P = 128
 C, S, N = 512, 1024, 2048
 BLOCKS = C // P
-PIECE = 512
+PIECE = 256
 PIECES = N // PIECE
+LOAD = 512
+LOADS = N // LOAD
 GROUPS = N // P
 IN_PIECE = PIECE // P
 EPS = 1e-5
@@ -21,7 +23,7 @@ def tile_proteintransformer_kernel(tc, tok, pos, gain, bias, offs, out):
     nc = tc.nc
     with (
         tc.tile_pool(name="held", bufs=1) as held,
-        tc.tile_pool(name="summed", bufs=2) as summed,
+        tc.tile_pool(name="summed", bufs=3) as summed,
         tc.tile_pool(name="stats", bufs=4) as stats,
         tc.tile_pool(name="normed", bufs=3) as normed,
         tc.tile_pool(name="result", bufs=4) as result,
@@ -44,18 +46,18 @@ def tile_proteintransformer_kernel(tc, tok, pos, gain, bias, offs, out):
         nc.sync.dma_start(offsets[:], offs)
         tok_sb = [held.tile([P, S], F32, name=f"tok{b}") for b in range(BLOCKS)]
         pos_sb = [
-            [held.tile([P, PIECE], F32, name=f"pos{b}_{k}") for k in range(PIECES)]
+            [held.tile([P, LOAD], F32, name=f"pos{b}_{k}") for k in range(LOADS)]
             for b in range(BLOCKS)
         ]
         for b in range(BLOCKS):
             nc.sync.dma_start(tok_sb[b][:], tok[b * P : (b + 1) * P, :])
-            nc.scalar.dma_start(pos_sb[b][0][:], pos[b * P : (b + 1) * P, 0:PIECE])
-        for k in range(1, PIECES):
+            nc.scalar.dma_start(pos_sb[b][0][:], pos[b * P : (b + 1) * P, 0:LOAD])
+        for k in range(1, LOADS):
             for b in range(BLOCKS):
                 queue = nc.sync if b % 2 == 0 else nc.scalar
                 queue.dma_start(
                     pos_sb[b][k][:],
-                    pos[b * P : (b + 1) * P, k * PIECE : (k + 1) * PIECE],
+                    pos[b * P : (b + 1) * P, k * LOAD : (k + 1) * LOAD],
                 )
 
         x, x_t, six, mean_var, neg_mean, rstd, shift, y_t, y, o = ({} for i in range(10))
@@ -66,7 +68,7 @@ def tile_proteintransformer_kernel(tc, tok, pos, gain, bias, offs, out):
             nc.vector.tensor_tensor(
                 x[k][b][:],
                 tok_sb[b][:].indirect(offsets[:, k * (PIECE // 16) : (k + 1) * (PIECE // 16)]),
-                pos_sb[b][k][:],
+                pos_sb[b][k * PIECE // LOAD][:, k * PIECE % LOAD : k * PIECE % LOAD + PIECE],
                 ADD,
             )
 
@@ -112,7 +114,8 @@ def tile_proteintransformer_kernel(tc, tok, pos, gain, bias, offs, out):
                 six[measuring] = stats.tile([P, 6], F32, name="six")
                 nc.vector.bn_stats(six[measuring][:], x_t[measuring][:])
             if turn < GROUPS - IN_PIECE:
-                look_up(turn // IN_PIECE + 1, turn % IN_PIECE)
+                for i in range(BLOCKS // IN_PIECE):
+                    look_up(turn // IN_PIECE + 1, turn % IN_PIECE * (BLOCKS // IN_PIECE) + i)
             if 0 <= measuring < GROUPS:
                 mean_var[measuring] = stats.tile([P, 2], F32, name="mean_var")
                 nc.vector.bn_aggr(mean_var[measuring][:], six[measuring][:])

@@ -4,6 +4,7 @@ from concourse.masks import make_identity
 F32 = mybir.dt.float32
 U16 = mybir.dt.uint16
 ADD = mybir.AluOpType.add
+MULT = mybir.AluOpType.mult
 IDENTITY = mybir.ActivationFunctionType.Identity
 RSQRT = mybir.ActivationFunctionType.Abs_reciprocal_sqrt
 
@@ -24,11 +25,11 @@ def tile_proteintransformer_kernel(tc, tok, pos, gain, bias, offs, out):
     with (
         tc.tile_pool(name="held", bufs=1) as held,
         tc.tile_pool(name="summed", bufs=3) as summed,
-        tc.tile_pool(name="stats", bufs=4) as stats,
-        tc.tile_pool(name="normed", bufs=3) as normed,
-        tc.tile_pool(name="result", bufs=4) as result,
-        tc.psum_pool(name="flipped", bufs=4) as flipped,
-        tc.psum_pool(name="restored", bufs=4) as restored,
+        tc.tile_pool(name="stats", bufs=8) as stats,
+        tc.tile_pool(name="normed", bufs=6) as normed,
+        tc.tile_pool(name="result", bufs=8) as result,
+        tc.psum_pool(name="flipped", bufs=5) as flipped,
+        tc.psum_pool(name="restored", bufs=3) as restored,
     ):
         identity = held.tile([P, P], F32, name="identity")
         make_identity(nc, identity[:])
@@ -85,14 +86,24 @@ def tile_proteintransformer_kernel(tc, tok, pos, gain, bias, offs, out):
             for b in range(BLOCKS):
                 nc.tensor.transpose(y[g][:, b, :], y_t[g][:, b * P : (b + 1) * P], identity[:])
 
-        def gain_and_bias(g, b):
-            nc.scalar.activation(
-                o[g][:, b, :],
-                y[g][:, b, :],
-                IDENTITY,
-                bias=affine[:, BLOCKS + b : BLOCKS + b + 1],
-                scale=affine[:, b : b + 1],
-            )
+        def gain_and_bias(g, b, engine):
+            if engine is nc.scalar:
+                nc.scalar.activation(
+                    o[g][:, b, :],
+                    y[g][:, b, :],
+                    IDENTITY,
+                    bias=affine[:, BLOCKS + b : BLOCKS + b + 1],
+                    scale=affine[:, b : b + 1],
+                )
+            else:
+                nc.vector.tensor_scalar(
+                    out=o[g][:, b, :],
+                    in0=y[g][:, b, :],
+                    scalar1=affine[:, b : b + 1],
+                    scalar2=affine[:, BLOCKS + b : BLOCKS + b + 1],
+                    op0=MULT,
+                    op1=ADD,
+                )
 
         for b in range(BLOCKS):
             look_up(0, b)
@@ -127,16 +138,17 @@ def tile_proteintransformer_kernel(tc, tok, pos, gain, bias, offs, out):
                 nc.scalar.activation(rstd[scaling][:], mean_var[scaling][:, 1:2], RSQRT, bias=eps[:])
             if 0 <= finishing < GROUPS:
                 o[finishing] = result.tile([P, BLOCKS, P], F32, name="o")
-                gain_and_bias(finishing, 0)
-                gain_and_bias(finishing, 1)
+                gain_and_bias(finishing, 0, nc.scalar)
+                gain_and_bias(finishing, 1, nc.scalar)
             if 0 <= scaling < GROUPS:
                 shift[scaling] = stats.tile([P, 1], F32, name="shift")
                 nc.scalar.activation(
                     shift[scaling][:], neg_mean[scaling][:], IDENTITY, scale=rstd[scaling][:]
                 )
             if 0 <= finishing < GROUPS:
-                gain_and_bias(finishing, 2)
-                gain_and_bias(finishing, 3)
+                helper = nc.vector if turn >= GROUPS - IN_PIECE else nc.scalar
+                gain_and_bias(finishing, 2, helper)
+                gain_and_bias(finishing, 3, helper)
                 nc.sync.dma_start(
                     out[:, finishing * P : (finishing + 1) * P].rearrange("(b p) j -> p b j", p=P),
                     o[finishing][:],

@@ -148,7 +148,7 @@ def tile_proteintransformer_kernel(tc, tok, pos, gain, bias, offs, out):
             if 0 <= finishing < GROUPS:
                 helper = nc.vector if turn >= GROUPS - IN_PIECE else nc.scalar
                 gain_and_bias(finishing, 2, helper)
-                gain_and_bias(finishing, 3, helper)
+                gain_and_bias(finishing, 3, nc.vector)
                 nc.sync.dma_start(
                     out[:, finishing * P : (finishing + 1) * P].rearrange("(b p) j -> p b j", p=P),
                     o[finishing][:],

@@ -38,10 +38,6 @@ def tile_proteintransformer_kernel(tc, tok, pos, gain, bias, offs, out):
 
         rows = held.tile([P, P], F32, name="rows")
         nc.gpsimd.memset(rows[:], 0.0)
-        nc.scalar.dma_start(rows[0:BLOCKS, :], gain.rearrange("(b p) o -> b (p o)", p=P))
-        nc.scalar.dma_start(
-            rows[BLOCKS : 2 * BLOCKS, :], bias.rearrange("(b p) o -> b (p o)", p=P)
-        )
 
         offsets = held.tile([P, N // 16], U16, name="offsets")
         nc.sync.dma_start(offsets[:], offs)
@@ -51,12 +47,15 @@ def tile_proteintransformer_kernel(tc, tok, pos, gain, bias, offs, out):
             for b in range(BLOCKS)
         ]
         for b in range(BLOCKS):
-            nc.sync.dma_start(tok_sb[b][:], tok[b * P : (b + 1) * P, :])
-            nc.scalar.dma_start(pos_sb[b][0][:], pos[b * P : (b + 1) * P, 0:LOAD])
-        for k in range(1, LOADS):
+            nc.scalar.dma_start(tok_sb[b][:], tok[b * P : (b + 1) * P, :])
+            if b == 1:
+                nc.scalar.dma_start(rows[0:BLOCKS, :], gain.rearrange("(b p) o -> b (p o)", p=P))
+                nc.scalar.dma_start(
+                    rows[BLOCKS : 2 * BLOCKS, :], bias.rearrange("(b p) o -> b (p o)", p=P)
+                )
+        for k in range(LOADS):
             for b in range(BLOCKS):
-                queue = nc.sync if b % 2 == 0 else nc.scalar
-                queue.dma_start(
+                nc.sync.dma_start(
                     pos_sb[b][k][:],
                     pos[b * P : (b + 1) * P, k * LOAD : (k + 1) * LOAD],
                 )

@@ -13,7 +13,7 @@ C, S, N = 512, 1024, 2048
 BLOCKS = C // P
 PIECE = 256
 PIECES = N // PIECE
-LOAD = 512
+LOAD = 256
 LOADS = N // LOAD
 GROUPS = N // P
 IN_PIECE = PIECE // P

@@ -17,6 +17,7 @@ LOAD = 256
 LOADS = N // LOAD
 GROUPS = N // P
 IN_PIECE = PIECE // P
+LEAD = 2
 EPS = 1e-5
 
 
@@ -24,7 +25,7 @@ def tile_proteintransformer_kernel(tc, tok, pos, gain, bias, offs, out):
     nc = tc.nc
     with (
         tc.tile_pool(name="held", bufs=1) as held,
-        tc.tile_pool(name="summed", bufs=3) as summed,
+        tc.tile_pool(name="summed", bufs=4) as summed,
         tc.tile_pool(name="stats", bufs=8) as stats,
         tc.tile_pool(name="normed", bufs=6) as normed,
         tc.tile_pool(name="result", bufs=8) as result,
@@ -53,20 +54,22 @@ def tile_proteintransformer_kernel(tc, tok, pos, gain, bias, offs, out):
                 nc.scalar.dma_start(
                     rows[BLOCKS : 2 * BLOCKS, :], bias.rearrange("(b p) o -> b (p o)", p=P)
                 )
-        for k in range(LOADS):
+        def load_pos(k, b):
+            nc.sync.dma_start(pos_sb[b][k][:], pos[b * P : (b + 1) * P, k * LOAD : (k + 1) * LOAD])
+
+        for b in range(BLOCKS):
+            for k in range(LEAD + 1):
+                load_pos(k, b)
+        for k in range(LEAD + 1, LOADS):
             for b in range(BLOCKS):
-                nc.sync.dma_start(
-                    pos_sb[b][k][:],
-                    pos[b * P : (b + 1) * P, k * LOAD : (k + 1) * LOAD],
-                )
+                load_pos(k, b)
 
         x, x_t, six, mean_var, neg_mean, rstd, shift, y_t, y, o = ({} for i in range(10))
 
         def look_up(k, b):
-            if b == 0:
-                x[k] = [summed.tile([P, PIECE], F32, name=f"x{i}") for i in range(BLOCKS)]
+            x[k, b] = summed.tile([P, PIECE], F32, name=f"x{b}")
             nc.vector.tensor_tensor(
-                x[k][b][:],
+                x[k, b][:],
                 tok_sb[b][:].indirect(offsets[:, k * (PIECE // 16) : (k + 1) * (PIECE // 16)]),
                 pos_sb[b][k * PIECE // LOAD][:, k * PIECE % LOAD : k * PIECE % LOAD + PIECE],
                 ADD,
@@ -77,7 +80,7 @@ def tile_proteintransformer_kernel(tc, tok, pos, gain, bias, offs, out):
             x_t[g] = flipped.tile([P, C], F32, name="x_t")
             for b in range(BLOCKS):
                 nc.tensor.transpose(
-                    x_t[g][:, b * P : (b + 1) * P], x[g // IN_PIECE][b][:, cols], identity[:]
+                    x_t[g][:, b * P : (b + 1) * P], x[g // IN_PIECE, b][:, cols], identity[:]
                 )
 
         def flip_back(g):
@@ -105,7 +108,8 @@ def tile_proteintransformer_kernel(tc, tok, pos, gain, bias, offs, out):
                 )
 
         for b in range(BLOCKS):
-            look_up(0, b)
+            for k in range(LEAD):
+                look_up(k, b)
 
         rows_t = flipped.tile([P, P], F32, name="rows_t", tag="x_t")
         nc.tensor.transpose(rows_t[:], rows[:], identity[:])
@@ -123,9 +127,9 @@ def tile_proteintransformer_kernel(tc, tok, pos, gain, bias, offs, out):
             if 0 <= measuring < GROUPS:
                 six[measuring] = stats.tile([P, 6], F32, name="six")
                 nc.vector.bn_stats(six[measuring][:], x_t[measuring][:])
-            if turn < GROUPS - IN_PIECE:
+            if turn < GROUPS - LEAD * IN_PIECE:
                 for i in range(BLOCKS // IN_PIECE):
-                    look_up(turn // IN_PIECE + 1, turn % IN_PIECE * (BLOCKS // IN_PIECE) + i)
+                    look_up(turn // IN_PIECE + LEAD, turn % IN_PIECE * (BLOCKS // IN_PIECE) + i)
             if 0 <= measuring < GROUPS:
                 mean_var[measuring] = stats.tile([P, 2], F32, name="mean_var")
                 nc.vector.bn_aggr(mean_var[measuring][:], six[measuring][:])
@@ -145,7 +149,7 @@ def tile_proteintransformer_kernel(tc, tok, pos, gain, bias, offs, out):
                     shift[scaling][:], neg_mean[scaling][:], IDENTITY, scale=rstd[scaling][:]
                 )
             if 0 <= finishing < GROUPS:
-                helper = nc.vector if turn >= GROUPS - IN_PIECE else nc.scalar
+                helper = nc.vector if turn >= GROUPS - LEAD * IN_PIECE else nc.scalar
                 gain_and_bias(finishing, 2, helper)
                 gain_and_bias(finishing, 3, nc.vector)
                 nc.sync.dma_start(

@@ -151,7 +151,7 @@ def tile_proteintransformer_kernel(tc, tok, pos, gain, bias, offs, out):
             if 0 <= finishing < GROUPS:
                 helper = nc.vector if turn >= GROUPS - LEAD * IN_PIECE else nc.scalar
                 gain_and_bias(finishing, 2, helper)
-                gain_and_bias(finishing, 3, nc.vector)
+                gain_and_bias(finishing, 3, helper)
                 nc.sync.dma_start(
                     out[:, finishing * P : (finishing + 1) * P].rearrange("(b p) j -> p b j", p=P),
                     o[finishing][:],

@@ -18,6 +18,7 @@ LOADS = N // LOAD
 GROUPS = N // P
 IN_PIECE = PIECE // P
 LEAD = 2
+LATE = GROUPS - 4
 EPS = 1e-5
 
 
@@ -84,15 +85,18 @@ def tile_proteintransformer_kernel(tc, tok, pos, gain, bias, offs, out):
                 )
 
         def flip_back(g):
-            y[g] = restored.tile([P, BLOCKS, P], F32, name="y")
+            in_bank = BLOCKS // 2 if g >= LATE else BLOCKS
             for b in range(BLOCKS):
-                nc.tensor.transpose(y[g][:, b, :], y_t[g][:, b * P : (b + 1) * P], identity[:])
+                if b % in_bank == 0:
+                    bank = restored.tile([P, BLOCKS, P], F32, name="bank")
+                y[g, b] = bank[:, b, :]
+                nc.tensor.transpose(y[g, b], y_t[g][:, b * P : (b + 1) * P], identity[:])
 
         def gain_and_bias(g, b, engine):
             if engine is nc.scalar:
                 nc.scalar.activation(
                     o[g][:, b, :],
-                    y[g][:, b, :],
+                    y[g, b],
                     IDENTITY,
                     bias=affine[:, BLOCKS + b : BLOCKS + b + 1],
                     scale=affine[:, b : b + 1],
@@ -100,12 +104,18 @@ def tile_proteintransformer_kernel(tc, tok, pos, gain, bias, offs, out):
             else:
                 nc.vector.tensor_scalar(
                     out=o[g][:, b, :],
-                    in0=y[g][:, b, :],
+                    in0=y[g, b],
                     scalar1=affine[:, b : b + 1],
                     scalar2=affine[:, BLOCKS + b : BLOCKS + b + 1],
                     op0=MULT,
                     op1=ADD,
                 )
+
+        def store(g, first, last):
+            nc.sync.dma_start(
+                out[first * P : last * P, g * P : (g + 1) * P].rearrange("(b p) j -> p b j", p=P),
+                o[g][:, first:last, :],
+            )
 
         for b in range(BLOCKS):
             for k in range(LEAD):
@@ -139,29 +149,31 @@ def tile_proteintransformer_kernel(tc, tok, pos, gain, bias, offs, out):
                 nc.scalar.mul(neg_mean[scaling][:], mean_var[scaling][:, 0:1], -1.0)
                 rstd[scaling] = stats.tile([P, 1], F32, name="rstd")
                 nc.scalar.activation(rstd[scaling][:], mean_var[scaling][:, 1:2], RSQRT, bias=eps[:])
+            late = finishing >= LATE
             if 0 <= finishing < GROUPS:
                 o[finishing] = result.tile([P, BLOCKS, P], F32, name="o")
-                gain_and_bias(finishing, 0, nc.scalar)
-                gain_and_bias(finishing, 1, nc.scalar)
+                helper = nc.vector if late else nc.scalar
+                gain_and_bias(finishing, 0, helper)
+                gain_and_bias(finishing, 1, helper)
+                if late:
+                    store(finishing, 0, BLOCKS // 2)
             if 0 <= scaling < GROUPS:
                 shift[scaling] = stats.tile([P, 1], F32, name="shift")
                 nc.scalar.activation(
                     shift[scaling][:], neg_mean[scaling][:], IDENTITY, scale=rstd[scaling][:]
                 )
             if 0 <= finishing < GROUPS:
-                helper = nc.vector if turn >= GROUPS - LEAD * IN_PIECE else nc.scalar
-                gain_and_bias(finishing, 2, helper)
-                gain_and_bias(finishing, 3, helper)
-                nc.sync.dma_start(
-                    out[:, finishing * P : (finishing + 1) * P].rearrange("(b p) j -> p b j", p=P),
-                    o[finishing][:],
-                )
+                gain_and_bias(finishing, 2, nc.scalar)
+                gain_and_bias(finishing, 3, nc.scalar)
+                store(finishing, BLOCKS // 2 if late else 0, BLOCKS)
             if 0 <= scaling < GROUPS:
                 y_t[scaling] = normed.tile([P, C], F32, name="y_t")
-                nc.scalar.activation(
-                    y_t[scaling][:],
-                    x_t[scaling][:],
-                    IDENTITY,
-                    bias=shift[scaling][:],
-                    scale=rstd[scaling][:],
-                )
+                width = C // 2 if scaling >= LATE else C
+                for c in range(0, C, width):
+                    nc.scalar.activation(
+                        y_t[scaling][:, c : c + width],
+                        x_t[scaling][:, c : c + width],
+                        IDENTITY,
+                        bias=shift[scaling][:],
+                        scale=rstd[scaling][:],
+                    )

import concourse.mybir as mybir
from concourse.masks import make_identity

F32 = mybir.dt.float32
U16 = mybir.dt.uint16
ADD = mybir.AluOpType.add
MULT = mybir.AluOpType.mult
IDENTITY = mybir.ActivationFunctionType.Identity
RSQRT = mybir.ActivationFunctionType.Abs_reciprocal_sqrt

P = 128
C, S, N = 512, 1024, 2048
BLOCKS = C // P
PIECE = 256
PIECES = N // PIECE
LOAD = 256
LOADS = N // LOAD
GROUPS = N // P
IN_PIECE = PIECE // P
LEAD = 2
LATE = GROUPS - 4
EPS = 1e-5


def tile_proteintransformer_kernel(tc, tok, pos, gain, bias, offs, out):
    nc = tc.nc
    with (
        tc.tile_pool(name="held", bufs=1) as held,
        tc.tile_pool(name="summed", bufs=4) as summed,
        tc.tile_pool(name="stats", bufs=8) as stats,
        tc.tile_pool(name="normed", bufs=6) as normed,
        tc.tile_pool(name="result", bufs=8) as result,
        tc.psum_pool(name="flipped", bufs=5) as flipped,
        tc.psum_pool(name="restored", bufs=3) as restored,
    ):
        identity = held.tile([P, P], F32, name="identity")
        make_identity(nc, identity[:])
        eps = held.tile([P, 1], F32, name="eps")
        nc.gpsimd.memset(eps[:], EPS)

        rows = held.tile([P, P], F32, name="rows")
        nc.gpsimd.memset(rows[:], 0.0)

        offsets = held.tile([P, N // 16], U16, name="offsets")
        nc.sync.dma_start(offsets[:], offs)
        tok_sb = [held.tile([P, S], F32, name=f"tok{b}") for b in range(BLOCKS)]
        pos_sb = [
            [held.tile([P, LOAD], F32, name=f"pos{b}_{k}") for k in range(LOADS)]
            for b in range(BLOCKS)
        ]
        for b in range(BLOCKS):
            nc.scalar.dma_start(tok_sb[b][:], tok[b * P : (b + 1) * P, :])
            if b == 1:
                nc.scalar.dma_start(rows[0:BLOCKS, :], gain.rearrange("(b p) o -> b (p o)", p=P))
                nc.scalar.dma_start(
                    rows[BLOCKS : 2 * BLOCKS, :], bias.rearrange("(b p) o -> b (p o)", p=P)
                )
        def load_pos(k, b):
            nc.sync.dma_start(pos_sb[b][k][:], pos[b * P : (b + 1) * P, k * LOAD : (k + 1) * LOAD])

        for b in range(BLOCKS):
            for k in range(LEAD + 1):
                load_pos(k, b)
        for k in range(LEAD + 1, LOADS):
            for b in range(BLOCKS):
                load_pos(k, b)

        x, x_t, six, mean_var, neg_mean, rstd, shift, y_t, y, o = ({} for i in range(10))

        def look_up(k, b):
            x[k, b] = summed.tile([P, PIECE], F32, name=f"x{b}")
            nc.vector.tensor_tensor(
                x[k, b][:],
                tok_sb[b][:].indirect(offsets[:, k * (PIECE // 16) : (k + 1) * (PIECE // 16)]),
                pos_sb[b][k * PIECE // LOAD][:, k * PIECE % LOAD : k * PIECE % LOAD + PIECE],
                ADD,
            )

        def flip(g):
            cols = slice(g % IN_PIECE * P, (g % IN_PIECE + 1) * P)
            x_t[g] = flipped.tile([P, C], F32, name="x_t")
            for b in range(BLOCKS):
                nc.tensor.transpose(
                    x_t[g][:, b * P : (b + 1) * P], x[g // IN_PIECE, b][:, cols], identity[:]
                )

        def flip_back(g):
            in_bank = BLOCKS // 2 if g >= LATE else BLOCKS
            for b in range(BLOCKS):
                if b % in_bank == 0:
                    bank = restored.tile([P, BLOCKS, P], F32, name="bank")
                y[g, b] = bank[:, b, :]
                nc.tensor.transpose(y[g, b], y_t[g][:, b * P : (b + 1) * P], identity[:])

        def gain_and_bias(g, b, engine):
            if engine is nc.scalar:
                nc.scalar.activation(
                    o[g][:, b, :],
                    y[g, b],
                    IDENTITY,
                    bias=affine[:, BLOCKS + b : BLOCKS + b + 1],
                    scale=affine[:, b : b + 1],
                )
            else:
                nc.vector.tensor_scalar(
                    out=o[g][:, b, :],
                    in0=y[g, b],
                    scalar1=affine[:, b : b + 1],
                    scalar2=affine[:, BLOCKS + b : BLOCKS + b + 1],
                    op0=MULT,
                    op1=ADD,
                )

        def store(g, first, last):
            nc.sync.dma_start(
                out[first * P : last * P, g * P : (g + 1) * P].rearrange("(b p) j -> p b j", p=P),
                o[g][:, first:last, :],
            )

        for b in range(BLOCKS):
            for k in range(LEAD):
                look_up(k, b)

        rows_t = flipped.tile([P, P], F32, name="rows_t", tag="x_t")
        nc.tensor.transpose(rows_t[:], rows[:], identity[:])
        affine = held.tile([P, 2 * BLOCKS], F32, name="affine")
        nc.scalar.copy(affine[:], rows_t[:, 0 : 2 * BLOCKS])

        for turn in range(GROUPS + 4):
            flipping, measuring, scaling, restoring, finishing = (turn - i for i in range(5))

            if 0 <= restoring < GROUPS:
                flip_back(restoring)
            if flipping < GROUPS:
                flip(flipping)

            if 0 <= measuring < GROUPS:
                six[measuring] = stats.tile([P, 6], F32, name="six")
                nc.vector.bn_stats(six[measuring][:], x_t[measuring][:])
            if turn < GROUPS - LEAD * IN_PIECE:
                for i in range(BLOCKS // IN_PIECE):
                    look_up(turn // IN_PIECE + LEAD, turn % IN_PIECE * (BLOCKS // IN_PIECE) + i)
            if 0 <= measuring < GROUPS:
                mean_var[measuring] = stats.tile([P, 2], F32, name="mean_var")
                nc.vector.bn_aggr(mean_var[measuring][:], six[measuring][:])

            if 0 <= scaling < GROUPS:
                neg_mean[scaling] = stats.tile([P, 1], F32, name="neg_mean")
                nc.scalar.mul(neg_mean[scaling][:], mean_var[scaling][:, 0:1], -1.0)
                rstd[scaling] = stats.tile([P, 1], F32, name="rstd")
                nc.scalar.activation(rstd[scaling][:], mean_var[scaling][:, 1:2], RSQRT, bias=eps[:])
            late = finishing >= LATE
            if 0 <= finishing < GROUPS:
                o[finishing] = result.tile([P, BLOCKS, P], F32, name="o")
                helper = nc.vector if late else nc.scalar
                gain_and_bias(finishing, 0, helper)
                gain_and_bias(finishing, 1, helper)
                if late:
                    store(finishing, 0, BLOCKS // 2)
            if 0 <= scaling < GROUPS:
                shift[scaling] = stats.tile([P, 1], F32, name="shift")
                nc.scalar.activation(
                    shift[scaling][:], neg_mean[scaling][:], IDENTITY, scale=rstd[scaling][:]
                )
            if 0 <= finishing < GROUPS:
                gain_and_bias(finishing, 2, nc.scalar)
                gain_and_bias(finishing, 3, nc.scalar)
                store(finishing, BLOCKS // 2 if late else 0, BLOCKS)
            if 0 <= scaling < GROUPS:
                y_t[scaling] = normed.tile([P, C], F32, name="y_t")
                width = C // 2 if scaling >= LATE else C
                for c in range(0, C, width):
                    nc.scalar.activation(
                        y_t[scaling][:, c : c + width],
                        x_t[scaling][:, c : c + width],
                        IDENTITY,
                        bias=shift[scaling][:],
                        scale=rstd[scaling][:],
                    )
